import numpy as np
import ml_dtypes


def mxq(x, axis, fmt="e4m3"):
    dtype, down = {"e4m3": (ml_dtypes.float8_e4m3fn, 7), "e5m2": (ml_dtypes.float8_e5m2, 14)}[fmt]
    v = np.moveaxis(np.asarray(x, np.float32).astype(ml_dtypes.bfloat16).astype(np.float64), axis, -1)
    blocks = v.reshape(v.shape[:-1] + (-1, 32))
    amax = np.abs(blocks).max(-1, keepdims=True)
    byte = np.maximum(np.where(amax > 0, np.frexp(amax)[1] - 1 + 127, 0) - down, 1)
    scale = np.exp2(byte - 127.0)
    codes = (blocks / scale).astype(np.float32).astype(dtype).astype(np.float64)
    return np.moveaxis((codes * scale).reshape(v.shape), -1, axis)


WIDE = False


def mx_kscale(k):
    if not WIDE:
        return np.ones(k)
    levels = np.array([10, -10, 5, -5, 0])
    if k % 512:
        return np.exp2(np.random.permutation(np.resize(levels, k // 32))).repeat(32)
    a = np.empty((k // 512, 16))
    for p in range(k // 512):
        a[p, :8] = np.random.permutation(np.resize(levels, 8))
        for g in range(8):
            far = levels[np.abs(levels - a[p, g]) >= 10]
            a[p, g + 8] = far[np.random.randint(len(far))]
    return np.exp2(a.ravel()).repeat(32)


BF16 = ml_dtypes.bfloat16


def bf(x):
    return np.asarray(x, np.float32).astype(BF16)


def f64(x):
    return np.asarray(x).astype(np.float64)


B, CIN, COUT, E, G, NC = 2048, 512, 512, 4, 2, 2
OMEGA_0 = 30.0


def draw0():
    s = mx_kscale(CIN)
    wb = np.sqrt(6.0 / CIN) / OMEGA_0
    return {"in_feats": bf(np.random.standard_normal((B, CIN)) * s),
            "tile_gate": bf(np.random.standard_normal((B, E)) / np.sqrt(E)),
            "W": bf(np.random.uniform(-wb, wb, (E, COUT, CIN)) / s)}


def core(in_feats, tile_gate, W):
    xq = mxq(f64(in_feats), 1, "e4m3")
    wq = mxq(f64(W), 2, "e4m3")
    g = f64(tile_gate)
    out = np.zeros((B, COUT))
    for t in range(E):
        out = out + g[:, t:t + 1] * (xq @ wq[t].T)
    return np.sin(OMEGA_0 * out)


def e4m3fn_bytes(y):
    return np.clip(np.asarray(y, np.float64), -448.0, 448.0).astype(np.float32).astype(ml_dtypes.float8_e4m3fn).view(np.uint8)


def e4m3fn_values(b):
    return np.asarray(b, np.uint8).view(ml_dtypes.float8_e4m3fn).astype(np.float64)


def setup_inputs():
    d = draw0()
    x0 = np.asarray(d['in_feats']).astype(np.float64)
    s = (np.max(np.abs(x0), axis=(0,), keepdims=True) / 448.0).astype(np.float32)
    out = {}
    for k, v in d.items():
        if k == 'in_feats':
            out['in_feats_bytes'] = e4m3fn_bytes(x0 / s.astype(np.float64))
            out['in_feats_scale'] = s
        else:
            out[k] = v
    return out


def reference(in_feats_bytes, in_feats_scale, tile_gate, W):
    return core(e4m3fn_values(in_feats_bytes) * in_feats_scale.astype(np.float64), tile_gate, W)

@@ -1,0 +1,318 @@
+from contextlib import ExitStack
+import math
+
+import concourse.mybir as mybir
+import concourse.masks as masks
+
+F32 = mybir.dt.float32
+BF16 = mybir.dt.bfloat16
+U32 = mybir.dt.uint32
+U8 = mybir.dt.uint8
+I32 = mybir.dt.int32
+FP8 = mybir.dt.float8_e4m3fn
+FP8X4 = mybir.dt.float8_e4m3fn_x4
+ALU = mybir.AluOpType
+ACT = mybir.ActivationFunctionType
+ENG = mybir.EngineType
+
+B, CIN, COUT, E = 2048, 512, 512, 4
+P = 128
+NT = B // P
+NQ = NT // 2
+FLOPS = 2 * B * CIN * COUT * E
+
+TURNS = 30.0 / (2.0 * math.pi)
+TWO_PI = 2.0 * math.pi
+VPAIRS = 3
+PE_BCAST = False
+HEAD = "x"
+X_CHUNKS = ((0, 2), (2, 6), (6, 10), (10, 16))
+
+
+def tile_sinelayer_loe_pa_kernel(tc, in_feats_bytes, in_feats_scale, tile_gate, W, out):
+    nc = tc.nc
+    with ExitStack() as ctx:
+        const = ctx.enter_context(tc.tile_pool(name="const", bufs=1))
+        grp = ctx.enter_context(tc.tile_pool(name="grp", bufs=3))
+        work = ctx.enter_context(tc.tile_pool(name="work", bufs=3))
+        psum = ctx.enter_context(tc.psum_pool(name="psum", bufs=8))
+
+        x_view = in_feats_bytes.rearrange("(p n) k -> p n k", n=NT)
+        out_view = out.rearrange("(p n) c -> p n c", n=NT)
+
+        g_bf = const.tile([P, NT * E], BF16, name="g_bf")
+        sc = const.tile([P, CIN], F32, name="sc")
+        if PE_BCAST:
+            scrow = const.tile([P, CIN], F32, name="scrow")
+            nc.vector.memset(scrow[:], 0.0)
+            ones = const.tile([P, P], F32, name="ones")
+            nc.vector.memset(ones[:], 1.0)
+            nc.scalar.dma_start(out=scrow[0:1, :], in_=in_feats_scale)
+        else:
+            nc.scalar.dma_start(out=sc[:], in_=in_feats_scale.rearrange("o k -> (o k)").partition_broadcast(P))
+        nc.scalar.dma_start(out=g_bf[:], in_=tile_gate.rearrange("(p n) e -> p (n e)", n=NT))
+
+        xbytes = []
+        for c in range(4):
+            lo, hi = X_CHUNKS[c]
+            xb = const.tile([P, hi - lo, CIN], U8, name="xbytes%d" % c)
+            xbytes.append(xb)
+        w_sb = []
+        for t in range(E):
+            ws = const.tile([P, 4, CIN], BF16, name="w_sb%d" % t)
+            w_sb.append(ws)
+
+        def load_x(c):
+            lo, hi = X_CHUNKS[c]
+            nc.sync.dma_start(out=xbytes[c][:], in_=x_view[:, lo:hi, :])
+
+        def load_w(t, a0=0, a1=4):
+            nc.sync.dma_start(out=w_sb[t][:, a0:a1, :], in_=W[t].rearrange("(a r) k -> r a k", r=P)[:, a0:a1, :])
+
+        if HEAD == "x":
+            load_x(0)
+            load_w(0)
+            load_x(1)
+            load_w(1)
+        else:
+            load_w(0, 0, 2)
+            load_w(0, 2, 4)
+            load_w(1)
+            load_x(0)
+            load_x(1)
+        load_w(2)
+        load_w(3)
+        load_x(2)
+        load_x(3)
+
+        warm = const.tile([P, 1], F32, name="warm")
+        nc.vector.memset(warm[:], 0.0)
+        warm2 = const.tile([P, 1], F32, name="warm2")
+        nc.scalar.activation(out=warm2[:], in_=warm[:], func=ACT.Sin)
+
+        ident = const.tile([P, P], F32, name="ident")
+        masks.make_identity(nc, ident[:])
+
+        gs = const.tile([P, NT * E], F32, name="gs")
+
+        xcodes = const.tile([P, B], U32, name="xcodes", align_bytes=64)
+        xscales = const.tile([P, B], U8, name="xscales", align_bytes=64)
+        wcodes = const.tile([P, E * COUT], U32, name="wcodes", align_bytes=64)
+        wscales = const.tile([P, E * COUT], U8, name="wscales", align_bytes=64)
+
+        def bank():
+            pm = psum.tile([P, COUT], F32, name="pm", tag="pm")
+            return pm
+
+        def turn(src_words, dst_words, eng):
+            tr = bank()
+            trv = tr[:].rearrange("p (j u r) -> p j u r", j=2, u=2)
+            for j in range(2):
+                for u in range(2):
+                    nc.tensor.transpose(trv[:, j, u, :], src_words[:, 256 * j + u:256 * j + 256:2], ident[:])
+            if eng == "V":
+                nc.vector.tensor_copy(out=dst_words, in_=trv.rearrange("p j u r -> p j r u"))
+            else:
+                nc.scalar.copy(out=dst_words, in_=trv.rearrange("p j u r -> p j r u"))
+
+        wgs = {}
+
+        def w_turn(t, h, eng):
+            if h == 0:
+                wg = grp.tile([P, 4 * COUT], BF16, name="wg", tag="wg", bufs=2, align_bytes=64)
+                wgs[t] = wg
+            src_words = w_sb[t][:].rearrange("p a k -> p (a k)").bitcast(F32)
+            dst_words = wgs[t][:].bitcast(F32).rearrange("p (j r u) -> p j r u", j=4, u=2)
+            turn(src_words[:, 512 * h:512 * h + 512], dst_words[:, 2 * h:2 * h + 2, :, :], eng)
+
+        def w_quant(t):
+            cols = slice(t * COUT, (t + 1) * COUT)
+            nc.vector.quantize_mx(out=wcodes[:, cols].bitcast(FP8X4), scales=wscales[:, cols], in_=wgs[t][:])
+
+        xb16s = {}
+        xws = {}
+        xgs = {}
+
+        def pair_bytes(p):
+            for c in range(4):
+                lo, hi = X_CHUNKS[c]
+                if lo <= 2 * p < hi:
+                    return xbytes[c][:, 2 * p - lo:2 * p - lo + 2, :]
+            return None
+
+        def x_widen_v(p):
+            xw = grp.tile([P, 2, CIN], BF16, name="xw", tag="xw")
+            for j in range(2):
+                nc.vector.tensor_tensor(out=xw[:, j, :], in0=pair_bytes(p)[:, j, :].bitcast(FP8), in1=sc[:], op=ALU.mult)
+            xws[p] = xw
+
+        def x_cast_s(p):
+            xb16 = grp.tile([P, 2, CIN], BF16, name="xb16", tag="xb16", bufs=2)
+            nc.scalar.copy(out=xb16[:], in_=pair_bytes(p).bitcast(FP8))
+            xb16s[p] = xb16
+
+        def x_mult_g(p):
+            xw = grp.tile([P, 2, CIN], BF16, name="xw", tag="xw")
+            nc.gpsimd.tensor_tensor(out=xw[:], in0=xb16s[p][:], in1=sc[:].unsqueeze(1).to_broadcast([P, 2, CIN]), op=ALU.mult)
+            xws[p] = xw
+
+        def x_turn(p, eng="S"):
+            xg = grp.tile([P, 2 * 4 * P], BF16, name="xg", tag="xg", align_bytes=64)
+            src_words = xws[p][:].rearrange("p a k -> p (a k)").bitcast(F32)
+            dst_words = xg[:].bitcast(F32).rearrange("p (j r u) -> p j r u", j=2, u=2)
+            turn(src_words, dst_words, eng)
+            xgs[p] = xg
+
+        def x_quant(p):
+            cols = slice(p * 256, (p + 1) * 256)
+            nc.vector.quantize_mx(out=xcodes[:, cols].bitcast(FP8X4), scales=xscales[:, cols], in_=xgs[p][:])
+
+        def mm(n, t):
+            pm = bank()
+            xc = slice(n * P, (n + 1) * P)
+            wc = slice(t * COUT, (t + 1) * COUT)
+            nc.tensor.matmul_mx(out=pm[:], lhsT=xcodes[:, xc].bitcast(FP8X4), lhsT_scale=xscales[:, xc],
+                                rhs=wcodes[:, wc].bitcast(FP8X4), rhs_scale=wscales[:, wc],
+                                start=True, stop=True)
+            return pm
+
+        def gate(n, t):
+            return gs[:, E * n + t:E * n + t + 1]
+
+        accs = {}
+        kks = {}
+
+        def first_term(q):
+            acc = work.tile([P, 2, COUT], F32, name="acc", tag="acc", bufs=4)
+            accs[q] = acc
+            for j in range(2):
+                n = 2 * q + j
+                pm = mm(n, 0)
+                nc.scalar.activation(out=acc[:, j, :], in_=pm[:], func=ACT.Copy, scale=gate(n, 0))
+
+        def add_term(q, t, j):
+            n = 2 * q + j
+            pm = mm(n, t)
+            acc = accs[q]
+            nc.vector.scalar_tensor_tensor(out=acc[:, j, :], in0=pm[:], scalar=gate(n, t),
+                                           in1=acc[:, j, :], op0=ALU.mult, op1=ALU.add)
+
+        def add_terms(q, t):
+            add_term(q, t, 0)
+            add_term(q, t, 1)
+
+        def whole_turns_g(q):
+            kk = work.tile([P, 2, COUT], I32, name="kk", tag="kk", bufs=1)
+            nc.gpsimd.tensor_scalar(out=kk[:], in0=accs[q][:], scalar1=1.0, scalar2=0.0, op0=ALU.mult, op1=ALU.add)
+            kks[q] = kk
+
+        def finish(q):
+            rr = work.tile([P, 2, COUT], F32, name="rr", tag="rr", bufs=2)
+            nc.vector.tensor_tensor(out=rr[:], in0=accs[q][:], in1=kks[q][:], op=ALU.subtract)
+            oo = work.tile([P, 2, COUT], F32, name="oo", tag="oo")
+            nc.scalar.activation(out=oo[:], in_=rr[:], func=ACT.Sin, scale=TWO_PI)
+            nc.sync.dma_start(out=out_view[:, 2 * q:2 * q + 2, :], in_=oo[:])
+
+        def finish_tile(q, j, kt, c0, c1):
+            rr = work.tile([P, c1 - c0], F32, name="rt", tag="rt", bufs=3)
+            nc.vector.tensor_tensor(out=rr[:], in0=accs[q][:, j, c0:c1], in1=kt[:, c0:c1], op=ALU.subtract)
+            oo = work.tile([P, c1 - c0], F32, name="ot", tag="ot", bufs=3)
+            nc.scalar.activation(out=oo[:], in_=rr[:], func=ACT.Sin, scale=TWO_PI)
+            nc.sync.dma_start(out=out_view[:, 2 * q + j, c0:c1], in_=oo[:])
+
+        def turns_tile(q, j):
+            kt = work.tile([P, COUT], I32, name="kt", tag="kt", bufs=2)
+            nc.vector.tensor_copy(out=kt[:], in_=accs[q][:, j, :])
+            return kt
+
+        def spread_scales():
+            if PE_BCAST:
+                ps = bank()
+                nc.tensor.matmul(out=ps[:], lhsT=ones[:], rhs=scrow[:], start=True, stop=True)
+                nc.scalar.copy(out=sc[:], in_=ps[:])
+
+        with tc.manual_schedule(engines={ENG.DVE, ENG.Pool, ENG.Activation}):
+            if HEAD == "x":
+                spread_scales()
+                x_widen_v(0)
+                x_turn(0)
+                x_widen_v(1)
+                w_turn(0, 0, "S")
+                w_turn(0, 1, "S")
+                x_quant(0)
+                nc.vector.tensor_scalar(out=gs[:], in0=g_bf[:], scalar1=TURNS, scalar2=None, op0=ALU.mult)
+                x_widen_v(2)
+                w_quant(0)
+                x_turn(1)
+                w_turn(1, 0, "S")
+                w_turn(1, 1, "S")
+                w_quant(1)
+                x_quant(1)
+                first_term(0)
+                w_turn(2, 0, "V")
+                w_turn(2, 1, "S")
+                w_quant(2)
+                w_turn(3, 0, "V")
+                w_turn(3, 1, "S")
+                w_quant(3)
+                x_cast_s(3)
+            else:
+                w_turn(0, 0, "V")
+                nc.vector.tensor_scalar(out=gs[:], in0=g_bf[:], scalar1=TURNS, scalar2=None, op0=ALU.mult)
+                w_turn(0, 1, "S")
+                spread_scales()
+                w_quant(0)
+                w_turn(1, 0, "S")
+                w_turn(1, 1, "V")
+                w_quant(1)
+                x_widen_v(0)
+                x_turn(0)
+                x_widen_v(1)
+                w_turn(2, 0, "S")
+                w_turn(2, 1, "S")
+                x_quant(0)
+                x_turn(1)
+                x_widen_v(2)
+                w_quant(2)
+                first_term(0)
+                x_quant(1)
+                w_turn(3, 0, "S")
+                w_turn(3, 1, "V")
+                w_quant(3)
+                x_cast_s(3)
+
+            flag = const.tile([P, 16], U32, name="flag")
+            nc.gpsimd.tensor_copy(out=flag[:], in_=wcodes[:, E * COUT - 16:E * COUT])
+
+            for w in range(NQ):
+                last = w == NQ - 1
+                if w > 0:
+                    whole_turns_g(w - 1)
+                if VPAIRS <= w + 3 < NQ:
+                    x_mult_g(w + 3)
+                add_terms(w, 1)
+                if not last:
+                    first_term(w + 1)
+                add_terms(w, 2)
+                if last:
+                    finish(w - 1)
+                    add_term(w, 3, 0)
+                    add_term(w, 3, 1)
+                    k0 = turns_tile(w, 0)
+                    k1 = turns_tile(w, 1)
+                    finish_tile(w, 0, k0, 0, COUT)
+                    finish_tile(w, 1, k1, 0, COUT // 2)
+                    finish_tile(w, 1, k1, COUT // 2, COUT)
+                else:
+                    if w + 2 < NQ:
+                        x_turn(w + 2)
+                    add_term(w, 3, 0)
+                    if w == 0:
+                        x_quant(w + 2)
+                    add_term(w, 3, 1)
+                    if VPAIRS <= w + 4 < NQ:
+                        x_cast_s(w + 4)
+                    if 0 < w and w + 2 < NQ:
+                        x_quant(w + 2)
+                    if w > 0:
+                        finish(w - 1)

@@ -23,6 +23,7 @@ FLOPS = 2 * B * CIN * COUT * E
 
 TURNS = 30.0 / (2.0 * math.pi)
 TWO_PI = 2.0 * math.pi
+MAGIC = 12582912.0
 VPAIRS = 3
 PE_BCAST = False
 HEAD = "x"
@@ -203,14 +204,17 @@ def tile_sinelayer_loe_pa_kernel(tc, in_feats_bytes, in_feats_scale, tile_gate, 
 
         def whole_turns_g(q):
             kk = work.tile([P, 2, COUT], I32, name="kk", tag="kk", bufs=1)
-            nc.gpsimd.tensor_scalar(out=kk[:], in0=accs[q][:], scalar1=1.0, scalar2=0.0, op0=ALU.mult, op1=ALU.add)
+            nc.gpsimd.tensor_scalar(out=kk[:, 0, :], in0=accs[q][:, 0, :], scalar1=1.0, scalar2=MAGIC, op0=ALU.mult, op1=ALU.add)
             kks[q] = kk
+
+        def whole_turns_s(q):
+            nc.scalar.activation(out=kks[q][:, 1, :].bitcast(U32), in_=accs[q][:, 1, :], func=ACT.Copy, bias=MAGIC, scale=1.0)
 
         def finish(q):
             rr = work.tile([P, 2, COUT], F32, name="rr", tag="rr", bufs=2)
-            nc.vector.tensor_tensor(out=rr[:], in0=accs[q][:], in1=kks[q][:], op=ALU.subtract)
+            nc.vector.scalar_tensor_tensor(out=rr[:], in0=kks[q][:], scalar=MAGIC, in1=accs[q][:], op0=ALU.subtract, op1=ALU.subtract)
             oo = work.tile([P, 2, COUT], F32, name="oo", tag="oo")
-            nc.scalar.activation(out=oo[:], in_=rr[:], func=ACT.Sin, scale=TWO_PI)
+            nc.scalar.activation(out=oo[:], in_=rr[:], func=ACT.Sin, scale=-TWO_PI)
             nc.sync.dma_start(out=out_view[:, 2 * q:2 * q + 2, :], in_=oo[:])
 
         def finish_tile(q, j, kt, c0, c1):
@@ -291,6 +295,10 @@ def tile_sinelayer_loe_pa_kernel(tc, in_feats_bytes, in_feats_scale, tile_gate, 
                 if VPAIRS <= w + 3 < NQ:
                     x_mult_g(w + 3)
                 add_terms(w, 1)
+                if w + 2 < NQ:
+                    x_turn(w + 2)
+                if w > 0:
+                    whole_turns_s(w - 1)
                 if not last:
                     first_term(w + 1)
                 add_terms(w, 2)
@@ -304,8 +312,6 @@ def tile_sinelayer_loe_pa_kernel(tc, in_feats_bytes, in_feats_scale, tile_gate, 
                     finish_tile(w, 1, k1, 0, COUT // 2)
                     finish_tile(w, 1, k1, COUT // 2, COUT)
                 else:
-                    if w + 2 < NQ:
-                        x_turn(w + 2)
                     add_term(w, 3, 0)
                     if w == 0:
                         x_quant(w + 2)

@@ -25,8 +25,7 @@ TURNS = 30.0 / (2.0 * math.pi)
 TWO_PI = 2.0 * math.pi
 MAGIC = 12582912.0
 VPAIRS = 3
-PE_BCAST = False
-HEAD = "x"
+RRB = 3
 X_CHUNKS = ((0, 2), (2, 6), (6, 10), (10, 16))
 
 
@@ -43,14 +42,7 @@ def tile_sinelayer_loe_pa_kernel(tc, in_feats_bytes, in_feats_scale, tile_gate, 
 
         g_bf = const.tile([P, NT * E], BF16, name="g_bf")
         sc = const.tile([P, CIN], F32, name="sc")
-        if PE_BCAST:
-            scrow = const.tile([P, CIN], F32, name="scrow")
-            nc.vector.memset(scrow[:], 0.0)
-            ones = const.tile([P, P], F32, name="ones")
-            nc.vector.memset(ones[:], 1.0)
-            nc.scalar.dma_start(out=scrow[0:1, :], in_=in_feats_scale)
-        else:
-            nc.scalar.dma_start(out=sc[:], in_=in_feats_scale.rearrange("o k -> (o k)").partition_broadcast(P))
+        nc.scalar.dma_start(out=sc[:], in_=in_feats_scale.rearrange("o k -> (o k)").partition_broadcast(P))
         nc.scalar.dma_start(out=g_bf[:], in_=tile_gate.rearrange("(p n) e -> p (n e)", n=NT))
 
         xbytes = []
@@ -70,17 +62,10 @@ def tile_sinelayer_loe_pa_kernel(tc, in_feats_bytes, in_feats_scale, tile_gate, 
         def load_w(t, a0=0, a1=4):
             nc.sync.dma_start(out=w_sb[t][:, a0:a1, :], in_=W[t].rearrange("(a r) k -> r a k", r=P)[:, a0:a1, :])
 
-        if HEAD == "x":
-            load_x(0)
-            load_w(0)
-            load_x(1)
-            load_w(1)
-        else:
-            load_w(0, 0, 2)
-            load_w(0, 2, 4)
-            load_w(1)
-            load_x(0)
-            load_x(1)
+        load_x(0)
+        load_w(0)
+        load_x(1)
+        load_w(1)
         load_w(2)
         load_w(3)
         load_x(2)
@@ -211,7 +196,7 @@ def tile_sinelayer_loe_pa_kernel(tc, in_feats_bytes, in_feats_scale, tile_gate, 
             nc.scalar.activation(out=kks[q][:, 1, :].bitcast(U32), in_=accs[q][:, 1, :], func=ACT.Copy, bias=MAGIC, scale=1.0)
 
         def finish(q):
-            rr = work.tile([P, 2, COUT], F32, name="rr", tag="rr", bufs=2)
+            rr = work.tile([P, 2, COUT], F32, name="rr", tag="rr", bufs=RRB)
             nc.vector.scalar_tensor_tensor(out=rr[:], in0=kks[q][:], scalar=MAGIC, in1=accs[q][:], op0=ALU.subtract, op1=ALU.subtract)
             oo = work.tile([P, 2, COUT], F32, name="oo", tag="oo")
             nc.scalar.activation(out=oo[:], in_=rr[:], func=ACT.Sin, scale=-TWO_PI)
@@ -229,96 +214,187 @@ def tile_sinelayer_loe_pa_kernel(tc, in_feats_bytes, in_feats_scale, tile_gate, 
             nc.vector.tensor_copy(out=kt[:], in_=accs[q][:, j, :])
             return kt
 
-        def spread_scales():
-            if PE_BCAST:
-                ps = bank()
-                nc.tensor.matmul(out=ps[:], lhsT=ones[:], rhs=scrow[:], start=True, stop=True)
-                nc.scalar.copy(out=sc[:], in_=ps[:])
+        secs = {}
+        rrs = {}
+        early = {}
 
-        with tc.manual_schedule(engines={ENG.DVE, ENG.Pool, ENG.Activation}):
-            if HEAD == "x":
-                spread_scales()
-                x_widen_v(0)
-                x_turn(0)
-                x_widen_v(1)
-                w_turn(0, 0, "S")
-                w_turn(0, 1, "S")
-                x_quant(0)
-                nc.vector.tensor_scalar(out=gs[:], in0=g_bf[:], scalar1=TURNS, scalar2=None, op0=ALU.mult)
-                x_widen_v(2)
-                w_quant(0)
-                x_turn(1)
-                w_turn(1, 0, "S")
-                w_turn(1, 1, "S")
-                w_quant(1)
-                x_quant(1)
-                first_term(0)
-                w_turn(2, 0, "V")
-                w_turn(2, 1, "S")
-                w_quant(2)
-                w_turn(3, 0, "V")
-                w_turn(3, 1, "S")
-                w_quant(3)
-                x_cast_s(3)
-            else:
-                w_turn(0, 0, "V")
-                nc.vector.tensor_scalar(out=gs[:], in0=g_bf[:], scalar1=TURNS, scalar2=None, op0=ALU.mult)
-                w_turn(0, 1, "S")
-                spread_scales()
-                w_quant(0)
-                w_turn(1, 0, "S")
-                w_turn(1, 1, "V")
-                w_quant(1)
-                x_widen_v(0)
-                x_turn(0)
-                x_widen_v(1)
-                w_turn(2, 0, "S")
-                w_turn(2, 1, "S")
-                x_quant(0)
-                x_turn(1)
-                x_widen_v(2)
-                w_quant(2)
-                first_term(0)
-                x_quant(1)
-                w_turn(3, 0, "S")
-                w_turn(3, 1, "V")
-                w_quant(3)
-                x_cast_s(3)
+        def pre(q, t):
+            for j in range(2):
+                early[(q, t, j)] = mm(2 * q + j, t)
 
+        def add2(q, t):
+            for j in range(2):
+                n = 2 * q + j
+                pm = early[(q, t, j)] if (q, t, j) in early else mm(n, t)
+                nc.vector.scalar_tensor_tensor(out=accs[q][:, j, :], in0=pm[:], scalar=gate(n, t),
+                                               in1=accs[q][:, j, :], op0=ALU.mult, op1=ALU.add)
+
+        def second_term(q):
+            sec = work.tile([P, 2, COUT], F32, name="sec", tag="sec", bufs=2)
+            secs[q] = sec
+            for j in range(2):
+                n = 2 * q + j
+                pm = mm(n, 1)
+                nc.scalar.activation(out=sec[:, j, :], in_=pm[:], func=ACT.Copy, scale=gate(n, 1))
+
+        def new_sum(q):
+            vv = work.tile([P, 2, COUT], F32, name="vv", tag="vv", bufs=1)
+            olds[q] = accs[q]
+            accs[q] = vv
+
+        olds = {}
+
+        def join_g(q, j):
+            nc.gpsimd.tensor_tensor(out=accs[q][:, j, :], in0=olds[q][:, j, :], in1=secs[q][:, j, :], op=ALU.add)
+
+        def new_kk(q):
+            kk = work.tile([P, 2, COUT], I32, name="kk", tag="kk", bufs=1)
+            kks[q] = kk
+
+        def conv_g(q, j):
+            nc.gpsimd.tensor_scalar(out=kks[q][:, j, :], in0=accs[q][:, j, :], scalar1=1.0, scalar2=MAGIC, op0=ALU.mult, op1=ALU.add)
+
+        def conv_s(q, j):
+            nc.scalar.activation(out=kks[q][:, j, :].bitcast(U32), in_=accs[q][:, j, :], func=ACT.Copy, bias=MAGIC, scale=1.0)
+
+        def new_rr(q):
+            rr = work.tile([P, 2, COUT], F32, name="rr", tag="rr", bufs=RRB)
+            rrs[q] = rr
+
+        def sub_t(q, j):
+            nc.vector.scalar_tensor_tensor(out=rrs[q][:, j, :], in0=kks[q][:, j, :], scalar=MAGIC, in1=accs[q][:, j, :], op0=ALU.subtract, op1=ALU.subtract)
+
+        def sub_w(q):
+            nc.vector.scalar_tensor_tensor(out=rrs[q][:], in0=kks[q][:], scalar=MAGIC, in1=accs[q][:], op0=ALU.subtract, op1=ALU.subtract)
+
+        def sine(q):
+            oo = work.tile([P, 2, COUT], F32, name="oo", tag="oo")
+            nc.scalar.activation(out=oo[:], in_=rrs[q][:], func=ACT.Sin, scale=-TWO_PI)
+            nc.sync.dma_start(out=out_view[:, 2 * q:2 * q + 2, :], in_=oo[:])
+
+        def hold_g2(q):
+            flag2 = const.tile([P, 16], F32, name="flag2")
+            nc.gpsimd.tensor_copy(out=flag2[:], in_=rrs[q][:, 1, COUT - 16:COUT])
+
+        def gates():
+            nc.vector.tensor_scalar(out=gs[:], in0=g_bf[:], scalar1=TURNS, scalar2=None, op0=ALU.mult)
+
+        def hold_g():
             flag = const.tile([P, 16], U32, name="flag")
             nc.gpsimd.tensor_copy(out=flag[:], in_=wcodes[:, E * COUT - 16:E * COUT])
 
-            for w in range(NQ):
-                last = w == NQ - 1
+        with tc.manual_schedule(engines={ENG.DVE, ENG.Pool, ENG.Activation}):
+            x_widen_v(0)
+            x_turn(0)
+            x_widen_v(1)
+            w_turn(0, 0, "S")
+            w_turn(0, 1, "S")
+            x_quant(0)
+            gates()
+            x_widen_v(2)
+            w_quant(0)
+            x_turn(1)
+            w_turn(1, 0, "S")
+            w_turn(1, 1, "S")
+            w_quant(1)
+            x_quant(1)
+            first_term(0)
+            w_turn(2, 0, "V")
+            w_turn(2, 1, "S")
+            w_quant(2)
+            w_turn(3, 0, "V")
+            w_turn(3, 1, "S")
+            w_quant(3)
+            x_cast_s(3)
+            hold_g()
+
+            for w in range(4):
                 if w > 0:
-                    whole_turns_g(w - 1)
-                if VPAIRS <= w + 3 < NQ:
-                    x_mult_g(w + 3)
-                add_terms(w, 1)
-                if w + 2 < NQ:
-                    x_turn(w + 2)
+                    new_kk(w - 1)
+                    conv_g(w - 1, 0)
+                x_mult_g(w + 3)
+                add2(w, 1)
+                x_turn(w + 2)
                 if w > 0:
-                    whole_turns_s(w - 1)
-                if not last:
-                    first_term(w + 1)
-                add_terms(w, 2)
-                if last:
-                    finish(w - 1)
-                    add_term(w, 3, 0)
-                    add_term(w, 3, 1)
-                    k0 = turns_tile(w, 0)
-                    k1 = turns_tile(w, 1)
-                    finish_tile(w, 0, k0, 0, COUT)
-                    finish_tile(w, 1, k1, 0, COUT // 2)
-                    finish_tile(w, 1, k1, COUT // 2, COUT)
-                else:
-                    add_term(w, 3, 0)
-                    if w == 0:
-                        x_quant(w + 2)
-                    add_term(w, 3, 1)
-                    if VPAIRS <= w + 4 < NQ:
-                        x_cast_s(w + 4)
-                    if 0 < w and w + 2 < NQ:
-                        x_quant(w + 2)
-                    if w > 0:
-                        finish(w - 1)
+                    conv_s(w - 1, 1)
+                first_term(w + 1)
+                add2(w, 2)
+                add_term(w, 3, 0)
+                if w == 0:
+                    x_quant(w + 2)
+                add_term(w, 3, 1)
+                x_cast_s(w + 4)
+                if w == 3:
+                    pre(4, 2)
+                if w > 0:
+                    x_quant(w + 2)
+                if w == 3:
+                    first_term(5)
+                if w > 0:
+                    new_rr(w - 1)
+                    sub_w(w - 1)
+                if 0 < w < 3:
+                    sine(w - 1)
+            new_kk(3)
+            conv_g(3, 0)
+            x_mult_g(7)
+            add2(4, 2)
+            x_turn(6)
+            conv_s(3, 1)
+            add2(4, 3)
+            second_term(4)
+            add2(5, 2)
+            sine(2)
+            pre(5, 3)
+            x_quant(6)
+            first_term(6)
+            new_rr(3)
+            sub_w(3)
+
+            hold_g2(3)
+            new_sum(4)
+            join_g(4, 0)
+            join_g(4, 1)
+            new_kk(4)
+            add2(5, 3)
+            x_turn(7)
+            add2(6, 1)
+            second_term(5)
+            conv_s(4, 0)
+            add2(6, 2)
+            conv_s(4, 1)
+            pre(6, 3)
+            x_quant(7)
+            first_term(7)
+            new_rr(4)
+            sub_t(4, 0)
+            sub_t(4, 1)
+            sine(3)
+
+            new_sum(5)
+            join_g(5, 0)
+            join_g(5, 1)
+            new_kk(5)
+            add2(6, 3)
+            add2(7, 1)
+            conv_s(5, 0)
+            sine(4)
+            add2(7, 2)
+            conv_s(5, 1)
+            new_rr(5)
+            sub_t(5, 0)
+            sub_t(5, 1)
+
+            new_kk(6)
+            conv_g(6, 0)
+            add2(7, 3)
+            conv_s(6, 1)
+            sine(5)
+            new_rr(6)
+            sub_w(6)
+            sine(6)
+            k0 = turns_tile(7, 0)
+            k1 = turns_tile(7, 1)
+            finish_tile(7, 0, k0, 0, COUT)
+            finish_tile(7, 1, k1, 0, COUT // 2)
+            finish_tile(7, 1, k1, COUT // 2, COUT)

@@ -276,6 +276,31 @@ def tile_sinelayer_loe_pa_kernel(tc, in_feats_bytes, in_feats_scale, tile_gate, 
             flag2 = const.tile([P, 16], F32, name="flag2")
             nc.gpsimd.tensor_copy(out=flag2[:], in_=rrs[q][:, 1, COUT - 16:COUT])
 
+        def join01_g(q, j):
+            nc.gpsimd.tensor_tensor(out=accs[q][:, j, :], in0=accs[q][:, j, :], in1=secs[q][:, j, :], op=ALU.add)
+
+        def two_terms(q):
+            acc = work.tile([P, 2, COUT], F32, name="acc", tag="acc", bufs=4)
+            accs[q] = acc
+            sec = work.tile([P, 2, COUT], F32, name="sec", tag="sec", bufs=2)
+            secs[q] = sec
+            for j in range(2):
+                n = 2 * q + j
+                pm = mm(n, 0)
+                nc.scalar.activation(out=acc[:, j, :], in_=pm[:], func=ACT.Copy, scale=gate(n, 0))
+                pm = mm(n, 1)
+                nc.scalar.activation(out=sec[:, j, :], in_=pm[:], func=ACT.Copy, scale=gate(n, 1))
+
+        def add1(q, t, j):
+            n = 2 * q + j
+            pm = early[(q, t, j)] if (q, t, j) in early else mm(n, t)
+            nc.vector.scalar_tensor_tensor(out=accs[q][:, j, :], in0=pm[:], scalar=gate(n, t),
+                                           in1=accs[q][:, j, :], op0=ALU.mult, op1=ALU.add)
+
+        def new_kk6(q):
+            kk = work.tile([P, 2, COUT], I32, name="kk6", tag="kk6", bufs=1)
+            kks[q] = kk
+
         def gates():
             nc.vector.tensor_scalar(out=gs[:], in0=g_bf[:], scalar1=TURNS, scalar2=None, op0=ALU.mult)
 
@@ -368,6 +393,7 @@ def tile_sinelayer_loe_pa_kernel(tc, in_feats_bytes, in_feats_scale, tile_gate, 
             first_term(7)
             new_rr(4)
             sub_t(4, 0)
+            add1(6, 3, 0)
             sub_t(4, 1)
             sine(3)
 
@@ -375,24 +401,25 @@ def tile_sinelayer_loe_pa_kernel(tc, in_feats_bytes, in_feats_scale, tile_gate, 
             join_g(5, 0)
             join_g(5, 1)
             new_kk(5)
-            add2(6, 3)
+            add1(6, 3, 1)
+            new_kk6(6)
+            conv_s(6, 0)
+            conv_s(6, 1)
             add2(7, 1)
             conv_s(5, 0)
-            sine(4)
             add2(7, 2)
             conv_s(5, 1)
-            new_rr(5)
-            sub_t(5, 0)
-            sub_t(5, 1)
-
-            new_kk(6)
-            conv_g(6, 0)
-            add2(7, 3)
-            conv_s(6, 1)
-            sine(5)
+            sine(4)
+            pre(7, 3)
             new_rr(6)
             sub_w(6)
             sine(6)
+            new_rr(5)
+            sub_t(5, 0)
+            sub_t(5, 1)
+            sine(5)
+            add1(7, 3, 0)
+            add1(7, 3, 1)
             k0 = turns_tile(7, 0)
             k1 = turns_tile(7, 1)
             finish_tile(7, 0, k0, 0, COUT)

@@ -318,17 +318,17 @@ def tile_sinelayer_loe_pa_kernel(tc, in_feats_bytes, in_feats_scale, tile_gate, 
             gates()
             x_widen_v(2)
             w_quant(0)
-            x_turn(1)
             w_turn(1, 0, "S")
             w_turn(1, 1, "S")
             w_quant(1)
-            x_quant(1)
-            first_term(0)
             w_turn(2, 0, "V")
             w_turn(2, 1, "S")
+            x_turn(1)
             w_quant(2)
+            first_term(0)
             w_turn(3, 0, "V")
             w_turn(3, 1, "S")
+            x_quant(1)
             w_quant(3)
             x_cast_s(3)
             hold_g()

@@ -338,16 +338,19 @@ def tile_sinelayer_loe_pa_kernel(tc, in_feats_bytes, in_feats_scale, tile_gate, 
                     new_kk(w - 1)
                     conv_g(w - 1, 0)
                 x_mult_g(w + 3)
+                pre(w, 1)
+                pre(w, 2)
+                pre(w, 3)
                 add2(w, 1)
                 x_turn(w + 2)
                 if w > 0:
                     conv_s(w - 1, 1)
                 first_term(w + 1)
                 add2(w, 2)
-                add_term(w, 3, 0)
+                add1(w, 3, 0)
                 if w == 0:
                     x_quant(w + 2)
-                add_term(w, 3, 1)
+                add1(w, 3, 1)
                 x_cast_s(w + 4)
                 if w == 3:
                     pre(4, 2)

@@ -366,6 +366,7 @@ def tile_sinelayer_loe_pa_kernel(tc, in_feats_bytes, in_feats_scale, tile_gate, 
             new_kk(3)
             conv_g(3, 0)
             x_mult_g(7)
+            pre(4, 3)
             add2(4, 2)
             x_turn(6)
             conv_s(3, 1)
@@ -384,6 +385,7 @@ def tile_sinelayer_loe_pa_kernel(tc, in_feats_bytes, in_feats_scale, tile_gate, 
             join_g(4, 0)
             join_g(4, 1)
             new_kk(4)
+            pre(6, 1)
             add2(5, 3)
             x_turn(7)
             add2(6, 1)

@@ -354,14 +354,13 @@ def tile_sinelayer_loe_pa_kernel(tc, in_feats_bytes, in_feats_scale, tile_gate, 
                 x_cast_s(w + 4)
                 if w == 3:
                     pre(4, 2)
-                if w > 0:
                     x_quant(w + 2)
-                if w == 3:
                     first_term(5)
                 if w > 0:
                     new_rr(w - 1)
                     sub_w(w - 1)
                 if 0 < w < 3:
+                    x_quant(w + 2)
                     sine(w - 1)
             new_kk(3)
             conv_g(3, 0)

from contextlib import ExitStack
import math

import concourse.mybir as mybir
import concourse.masks as masks

F32 = mybir.dt.float32
BF16 = mybir.dt.bfloat16
U32 = mybir.dt.uint32
U8 = mybir.dt.uint8
I32 = mybir.dt.int32
FP8 = mybir.dt.float8_e4m3fn
FP8X4 = mybir.dt.float8_e4m3fn_x4
ALU = mybir.AluOpType
ACT = mybir.ActivationFunctionType
ENG = mybir.EngineType

B, CIN, COUT, E = 2048, 512, 512, 4
P = 128
NT = B // P
NQ = NT // 2
FLOPS = 2 * B * CIN * COUT * E

TURNS = 30.0 / (2.0 * math.pi)
TWO_PI = 2.0 * math.pi
MAGIC = 12582912.0
VPAIRS = 3
RRB = 3
X_CHUNKS = ((0, 2), (2, 6), (6, 10), (10, 16))


def tile_sinelayer_loe_pa_kernel(tc, in_feats_bytes, in_feats_scale, tile_gate, W, out):
    nc = tc.nc
    with ExitStack() as ctx:
        const = ctx.enter_context(tc.tile_pool(name="const", bufs=1))
        grp = ctx.enter_context(tc.tile_pool(name="grp", bufs=3))
        work = ctx.enter_context(tc.tile_pool(name="work", bufs=3))
        psum = ctx.enter_context(tc.psum_pool(name="psum", bufs=8))

        x_view = in_feats_bytes.rearrange("(p n) k -> p n k", n=NT)
        out_view = out.rearrange("(p n) c -> p n c", n=NT)

        g_bf = const.tile([P, NT * E], BF16, name="g_bf")
        sc = const.tile([P, CIN], F32, name="sc")
        nc.scalar.dma_start(out=sc[:], in_=in_feats_scale.rearrange("o k -> (o k)").partition_broadcast(P))
        nc.scalar.dma_start(out=g_bf[:], in_=tile_gate.rearrange("(p n) e -> p (n e)", n=NT))

        xbytes = []
        for c in range(4):
            lo, hi = X_CHUNKS[c]
            xb = const.tile([P, hi - lo, CIN], U8, name="xbytes%d" % c)
            xbytes.append(xb)
        w_sb = []
        for t in range(E):
            ws = const.tile([P, 4, CIN], BF16, name="w_sb%d" % t)
            w_sb.append(ws)

        def load_x(c):
            lo, hi = X_CHUNKS[c]
            nc.sync.dma_start(out=xbytes[c][:], in_=x_view[:, lo:hi, :])

        def load_w(t, a0=0, a1=4):
            nc.sync.dma_start(out=w_sb[t][:, a0:a1, :], in_=W[t].rearrange("(a r) k -> r a k", r=P)[:, a0:a1, :])

        load_x(0)
        load_w(0)
        load_x(1)
        load_w(1)
        load_w(2)
        load_w(3)
        load_x(2)
        load_x(3)

        warm = const.tile([P, 1], F32, name="warm")
        nc.vector.memset(warm[:], 0.0)
        warm2 = const.tile([P, 1], F32, name="warm2")
        nc.scalar.activation(out=warm2[:], in_=warm[:], func=ACT.Sin)

        ident = const.tile([P, P], F32, name="ident")
        masks.make_identity(nc, ident[:])

        gs = const.tile([P, NT * E], F32, name="gs")

        xcodes = const.tile([P, B], U32, name="xcodes", align_bytes=64)
        xscales = const.tile([P, B], U8, name="xscales", align_bytes=64)
        wcodes = const.tile([P, E * COUT], U32, name="wcodes", align_bytes=64)
        wscales = const.tile([P, E * COUT], U8, name="wscales", align_bytes=64)

        def bank():
            pm = psum.tile([P, COUT], F32, name="pm", tag="pm")
            return pm

        def turn(src_words, dst_words, eng):
            tr = bank()
            trv = tr[:].rearrange("p (j u r) -> p j u r", j=2, u=2)
            for j in range(2):
                for u in range(2):
                    nc.tensor.transpose(trv[:, j, u, :], src_words[:, 256 * j + u:256 * j + 256:2], ident[:])
            if eng == "V":
                nc.vector.tensor_copy(out=dst_words, in_=trv.rearrange("p j u r -> p j r u"))
            else:
                nc.scalar.copy(out=dst_words, in_=trv.rearrange("p j u r -> p j r u"))

        wgs = {}

        def w_turn(t, h, eng):
            if h == 0:
                wg = grp.tile([P, 4 * COUT], BF16, name="wg", tag="wg", bufs=2, align_bytes=64)
                wgs[t] = wg
            src_words = w_sb[t][:].rearrange("p a k -> p (a k)").bitcast(F32)
            dst_words = wgs[t][:].bitcast(F32).rearrange("p (j r u) -> p j r u", j=4, u=2)
            turn(src_words[:, 512 * h:512 * h + 512], dst_words[:, 2 * h:2 * h + 2, :, :], eng)

        def w_quant(t):
            cols = slice(t * COUT, (t + 1) * COUT)
            nc.vector.quantize_mx(out=wcodes[:, cols].bitcast(FP8X4), scales=wscales[:, cols], in_=wgs[t][:])

        xb16s = {}
        xws = {}
        xgs = {}

        def pair_bytes(p):
            for c in range(4):
                lo, hi = X_CHUNKS[c]
                if lo <= 2 * p < hi:
                    return xbytes[c][:, 2 * p - lo:2 * p - lo + 2, :]
            return None

        def x_widen_v(p):
            xw = grp.tile([P, 2, CIN], BF16, name="xw", tag="xw")
            for j in range(2):
                nc.vector.tensor_tensor(out=xw[:, j, :], in0=pair_bytes(p)[:, j, :].bitcast(FP8), in1=sc[:], op=ALU.mult)
            xws[p] = xw

        def x_cast_s(p):
            xb16 = grp.tile([P, 2, CIN], BF16, name="xb16", tag="xb16", bufs=2)
            nc.scalar.copy(out=xb16[:], in_=pair_bytes(p).bitcast(FP8))
            xb16s[p] = xb16

        def x_mult_g(p):
            xw = grp.tile([P, 2, CIN], BF16, name="xw", tag="xw")
            nc.gpsimd.tensor_tensor(out=xw[:], in0=xb16s[p][:], in1=sc[:].unsqueeze(1).to_broadcast([P, 2, CIN]), op=ALU.mult)
            xws[p] = xw

        def x_turn(p, eng="S"):
            xg = grp.tile([P, 2 * 4 * P], BF16, name="xg", tag="xg", align_bytes=64)
            src_words = xws[p][:].rearrange("p a k -> p (a k)").bitcast(F32)
            dst_words = xg[:].bitcast(F32).rearrange("p (j r u) -> p j r u", j=2, u=2)
            turn(src_words, dst_words, eng)
            xgs[p] = xg

        def x_quant(p):
            cols = slice(p * 256, (p + 1) * 256)
            nc.vector.quantize_mx(out=xcodes[:, cols].bitcast(FP8X4), scales=xscales[:, cols], in_=xgs[p][:])

        def mm(n, t):
            pm = bank()
            xc = slice(n * P, (n + 1) * P)
            wc = slice(t * COUT, (t + 1) * COUT)
            nc.tensor.matmul_mx(out=pm[:], lhsT=xcodes[:, xc].bitcast(FP8X4), lhsT_scale=xscales[:, xc],
                                rhs=wcodes[:, wc].bitcast(FP8X4), rhs_scale=wscales[:, wc],
                                start=True, stop=True)
            return pm

        def gate(n, t):
            return gs[:, E * n + t:E * n + t + 1]

        accs = {}
        kks = {}

        def first_term(q):
            acc = work.tile([P, 2, COUT], F32, name="acc", tag="acc", bufs=4)
            accs[q] = acc
            for j in range(2):
                n = 2 * q + j
                pm = mm(n, 0)
                nc.scalar.activation(out=acc[:, j, :], in_=pm[:], func=ACT.Copy, scale=gate(n, 0))

        def add_term(q, t, j):
            n = 2 * q + j
            pm = mm(n, t)
            acc = accs[q]
            nc.vector.scalar_tensor_tensor(out=acc[:, j, :], in0=pm[:], scalar=gate(n, t),
                                           in1=acc[:, j, :], op0=ALU.mult, op1=ALU.add)

        def add_terms(q, t):
            add_term(q, t, 0)
            add_term(q, t, 1)

        def whole_turns_g(q):
            kk = work.tile([P, 2, COUT], I32, name="kk", tag="kk", bufs=1)
            nc.gpsimd.tensor_scalar(out=kk[:, 0, :], in0=accs[q][:, 0, :], scalar1=1.0, scalar2=MAGIC, op0=ALU.mult, op1=ALU.add)
            kks[q] = kk

        def whole_turns_s(q):
            nc.scalar.activation(out=kks[q][:, 1, :].bitcast(U32), in_=accs[q][:, 1, :], func=ACT.Copy, bias=MAGIC, scale=1.0)

        def finish(q):
            rr = work.tile([P, 2, COUT], F32, name="rr", tag="rr", bufs=RRB)
            nc.vector.scalar_tensor_tensor(out=rr[:], in0=kks[q][:], scalar=MAGIC, in1=accs[q][:], op0=ALU.subtract, op1=ALU.subtract)
            oo = work.tile([P, 2, COUT], F32, name="oo", tag="oo")
            nc.scalar.activation(out=oo[:], in_=rr[:], func=ACT.Sin, scale=-TWO_PI)
            nc.sync.dma_start(out=out_view[:, 2 * q:2 * q + 2, :], in_=oo[:])

        def finish_tile(q, j, kt, c0, c1):
            rr = work.tile([P, c1 - c0], F32, name="rt", tag="rt", bufs=3)
            nc.vector.tensor_tensor(out=rr[:], in0=accs[q][:, j, c0:c1], in1=kt[:, c0:c1], op=ALU.subtract)
            oo = work.tile([P, c1 - c0], F32, name="ot", tag="ot", bufs=3)
            nc.scalar.activation(out=oo[:], in_=rr[:], func=ACT.Sin, scale=TWO_PI)
            nc.sync.dma_start(out=out_view[:, 2 * q + j, c0:c1], in_=oo[:])

        def turns_tile(q, j):
            kt = work.tile([P, COUT], I32, name="kt", tag="kt", bufs=2)
            nc.vector.tensor_copy(out=kt[:], in_=accs[q][:, j, :])
            return kt

        secs = {}
        rrs = {}
        early = {}

        def pre(q, t):
            for j in range(2):
                early[(q, t, j)] = mm(2 * q + j, t)

        def add2(q, t):
            for j in range(2):
                n = 2 * q + j
                pm = early[(q, t, j)] if (q, t, j) in early else mm(n, t)
                nc.vector.scalar_tensor_tensor(out=accs[q][:, j, :], in0=pm[:], scalar=gate(n, t),
                                               in1=accs[q][:, j, :], op0=ALU.mult, op1=ALU.add)

        def second_term(q):
            sec = work.tile([P, 2, COUT], F32, name="sec", tag="sec", bufs=2)
            secs[q] = sec
            for j in range(2):
                n = 2 * q + j
                pm = mm(n, 1)
                nc.scalar.activation(out=sec[:, j, :], in_=pm[:], func=ACT.Copy, scale=gate(n, 1))

        def new_sum(q):
            vv = work.tile([P, 2, COUT], F32, name="vv", tag="vv", bufs=1)
            olds[q] = accs[q]
            accs[q] = vv

        olds = {}

        def join_g(q, j):
            nc.gpsimd.tensor_tensor(out=accs[q][:, j, :], in0=olds[q][:, j, :], in1=secs[q][:, j, :], op=ALU.add)

        def new_kk(q):
            kk = work.tile([P, 2, COUT], I32, name="kk", tag="kk", bufs=1)
            kks[q] = kk

        def conv_g(q, j):
            nc.gpsimd.tensor_scalar(out=kks[q][:, j, :], in0=accs[q][:, j, :], scalar1=1.0, scalar2=MAGIC, op0=ALU.mult, op1=ALU.add)

        def conv_s(q, j):
            nc.scalar.activation(out=kks[q][:, j, :].bitcast(U32), in_=accs[q][:, j, :], func=ACT.Copy, bias=MAGIC, scale=1.0)

        def new_rr(q):
            rr = work.tile([P, 2, COUT], F32, name="rr", tag="rr", bufs=RRB)
            rrs[q] = rr

        def sub_t(q, j):
            nc.vector.scalar_tensor_tensor(out=rrs[q][:, j, :], in0=kks[q][:, j, :], scalar=MAGIC, in1=accs[q][:, j, :], op0=ALU.subtract, op1=ALU.subtract)

        def sub_w(q):
            nc.vector.scalar_tensor_tensor(out=rrs[q][:], in0=kks[q][:], scalar=MAGIC, in1=accs[q][:], op0=ALU.subtract, op1=ALU.subtract)

        def sine(q):
            oo = work.tile([P, 2, COUT], F32, name="oo", tag="oo")
            nc.scalar.activation(out=oo[:], in_=rrs[q][:], func=ACT.Sin, scale=-TWO_PI)
            nc.sync.dma_start(out=out_view[:, 2 * q:2 * q + 2, :], in_=oo[:])

        def hold_g2(q):
            flag2 = const.tile([P, 16], F32, name="flag2")
            nc.gpsimd.tensor_copy(out=flag2[:], in_=rrs[q][:, 1, COUT - 16:COUT])

        def join01_g(q, j):
            nc.gpsimd.tensor_tensor(out=accs[q][:, j, :], in0=accs[q][:, j, :], in1=secs[q][:, j, :], op=ALU.add)

        def two_terms(q):
            acc = work.tile([P, 2, COUT], F32, name="acc", tag="acc", bufs=4)
            accs[q] = acc
            sec = work.tile([P, 2, COUT], F32, name="sec", tag="sec", bufs=2)
            secs[q] = sec
            for j in range(2):
                n = 2 * q + j
                pm = mm(n, 0)
                nc.scalar.activation(out=acc[:, j, :], in_=pm[:], func=ACT.Copy, scale=gate(n, 0))
                pm = mm(n, 1)
                nc.scalar.activation(out=sec[:, j, :], in_=pm[:], func=ACT.Copy, scale=gate(n, 1))

        def add1(q, t, j):
            n = 2 * q + j
            pm = early[(q, t, j)] if (q, t, j) in early else mm(n, t)
            nc.vector.scalar_tensor_tensor(out=accs[q][:, j, :], in0=pm[:], scalar=gate(n, t),
                                           in1=accs[q][:, j, :], op0=ALU.mult, op1=ALU.add)

        def new_kk6(q):
            kk = work.tile([P, 2, COUT], I32, name="kk6", tag="kk6", bufs=1)
            kks[q] = kk

        def gates():
            nc.vector.tensor_scalar(out=gs[:], in0=g_bf[:], scalar1=TURNS, scalar2=None, op0=ALU.mult)

        def hold_g():
            flag = const.tile([P, 16], U32, name="flag")
            nc.gpsimd.tensor_copy(out=flag[:], in_=wcodes[:, E * COUT - 16:E * COUT])

        with tc.manual_schedule(engines={ENG.DVE, ENG.Pool, ENG.Activation}):
            x_widen_v(0)
            x_turn(0)
            x_widen_v(1)
            w_turn(0, 0, "S")
            w_turn(0, 1, "S")
            x_quant(0)
            gates()
            x_widen_v(2)
            w_quant(0)
            w_turn(1, 0, "S")
            w_turn(1, 1, "S")
            w_quant(1)
            w_turn(2, 0, "V")
            w_turn(2, 1, "S")
            x_turn(1)
            w_quant(2)
            first_term(0)
            w_turn(3, 0, "V")
            w_turn(3, 1, "S")
            x_quant(1)
            w_quant(3)
            x_cast_s(3)
            hold_g()

            for w in range(4):
                if w > 0:
                    new_kk(w - 1)
                    conv_g(w - 1, 0)
                x_mult_g(w + 3)
                pre(w, 1)
                pre(w, 2)
                pre(w, 3)
                add2(w, 1)
                x_turn(w + 2)
                if w > 0:
                    conv_s(w - 1, 1)
                first_term(w + 1)
                add2(w, 2)
                add1(w, 3, 0)
                if w == 0:
                    x_quant(w + 2)
                add1(w, 3, 1)
                x_cast_s(w + 4)
                if w == 3:
                    pre(4, 2)
                    x_quant(w + 2)
                    first_term(5)
                if w > 0:
                    new_rr(w - 1)
                    sub_w(w - 1)
                if 0 < w < 3:
                    x_quant(w + 2)
                    sine(w - 1)
            new_kk(3)
            conv_g(3, 0)
            x_mult_g(7)
            pre(4, 3)
            add2(4, 2)
            x_turn(6)
            conv_s(3, 1)
            add2(4, 3)
            second_term(4)
            add2(5, 2)
            sine(2)
            pre(5, 3)
            x_quant(6)
            first_term(6)
            new_rr(3)
            sub_w(3)

            hold_g2(3)
            new_sum(4)
            join_g(4, 0)
            join_g(4, 1)
            new_kk(4)
            pre(6, 1)
            add2(5, 3)
            x_turn(7)
            add2(6, 1)
            second_term(5)
            conv_s(4, 0)
            add2(6, 2)
            conv_s(4, 1)
            pre(6, 3)
            x_quant(7)
            first_term(7)
            new_rr(4)
            sub_t(4, 0)
            add1(6, 3, 0)
            sub_t(4, 1)
            sine(3)

            new_sum(5)
            join_g(5, 0)
            join_g(5, 1)
            new_kk(5)
            add1(6, 3, 1)
            new_kk6(6)
            conv_s(6, 0)
            conv_s(6, 1)
            add2(7, 1)
            conv_s(5, 0)
            add2(7, 2)
            conv_s(5, 1)
            sine(4)
            pre(7, 3)
            new_rr(6)
            sub_w(6)
            sine(6)
            new_rr(5)
            sub_t(5, 0)
            sub_t(5, 1)
            sine(5)
            add1(7, 3, 0)
            add1(7, 3, 1)
            k0 = turns_tile(7, 0)
            k1 = turns_tile(7, 1)
            finish_tile(7, 0, k0, 0, COUT)
            finish_tile(7, 1, k1, 0, COUT // 2)
            finish_tile(7, 1, k1, COUT // 2, COUT)
